import numpy as np
import ml_dtypes


def mxq(x, axis, fmt="e4m3"):
    dtype, down = {"e4m3": (ml_dtypes.float8_e4m3fn, 7), "e5m2": (ml_dtypes.float8_e5m2, 14)}[fmt]
    v = np.moveaxis(np.asarray(x, np.float32).astype(ml_dtypes.bfloat16).astype(np.float64), axis, -1)
    blocks = v.reshape(v.shape[:-1] + (-1, 32))
    amax = np.abs(blocks).max(-1, keepdims=True)
    byte = np.maximum(np.where(amax > 0, np.frexp(amax)[1] - 1 + 127, 0) - down, 1)
    scale = np.exp2(byte - 127.0)
    codes = (blocks / scale).astype(np.float32).astype(dtype).astype(np.float64)
    return np.moveaxis((codes * scale).reshape(v.shape), -1, axis)


WIDE = False


def mx_kscale(k):
    if not WIDE:
        return np.ones(k)
    levels = np.array([10, -10, 5, -5, 0])
    a = np.random.permutation(np.resize(levels, k // 512 * 4)).reshape(k // 512, 4)
    idx = np.arange(k)
    return np.exp2(a[idx // 512, idx % 128 // 32])


BF16 = ml_dtypes.bfloat16


def bf(x):
    return np.asarray(x, np.float32).astype(BF16)


def f64(x):
    return np.asarray(x).astype(np.float64)


B, C, HH, WW, M, L, G, HID = 2, 1024, 8, 8, 128, 512, 256, 1024
N = HH * WW
ITERS = 3
DUST = 1.0


def lse(a, axis):
    top = a.max(axis=axis, keepdims=True)
    return np.log(np.exp(a - top).sum(axis=axis)) + np.squeeze(top, axis=axis)


def setup_inputs():
    s, t = mx_kscale(C), mx_kscale(HID)
    return {
        "x": bf(np.random.standard_normal((B, C, HH, WW)) * s[None, :, None, None]),
        "Ws1": bf(np.random.standard_normal((HID, C)) / np.sqrt(C) / s[None, :] * t[:, None]),
        "bs1": bf(np.random.standard_normal(HID) * 0.3 * t),
        "Ws2": bf(np.random.standard_normal((M, HID)) * 2.0 / np.sqrt(HID) / t[None, :]),
    }


def reference(x, Ws1, bs1, Ws2):
    xf = f64(x).reshape(B, C, N)
    hs = np.maximum((mxq(f64(Ws1), 1, "e4m3") @ mxq(xf, 1, "e4m3")) + f64(bs1)[None, :, None], 0.0)
    p = mxq(f64(Ws2), 1, "e4m3") @ mxq(hs, 1, "e4m3")
    norm = -np.log(M + N)
    log_mu = np.concatenate([np.full(M, norm), np.full(1, np.log(N) + norm)])
    log_nu = np.full(N, norm)
    Z = np.concatenate([p, np.full((B, 1, N), DUST)], axis=1)
    u = np.zeros((B, M + 1))
    v = np.zeros((B, N))
    for _ in range(ITERS):
        u = log_mu[None] - lse(Z + v[:, None, :], 2)
        v = log_nu[None] - lse(Z + u[:, :, None], 1)
    return np.exp(Z + u[:, :, None] + v[:, None, :] - norm)[:, :-1, :]

@@ -1,0 +1,209 @@
+from contextlib import ExitStack
+
+import concourse.mybir as mybir
+from concourse.masks import make_identity
+
+F32 = mybir.dt.float32
+BF16 = mybir.dt.bfloat16
+U32 = mybir.dt.uint32
+U8 = mybir.dt.uint8
+FP8X4 = mybir.dt.float8_e4m3fn_x4
+ACT = mybir.ActivationFunctionType
+ALU = mybir.AluOpType
+AXIS = mybir.AxisListType
+
+P = 128
+IMAGES = 2
+PIXELS = 64
+COLS = IMAGES * PIXELS
+K = 1024
+PACK = 4
+PASSES = K // (P * PACK)
+HALVES = 2
+ROW_TILES = K // P
+ROUNDS = 3
+W2_TURN = 2
+
+FLOPS = 2 * K * K * COLS + 2 * P * K * COLS
+
+
+def tile_salad_pa_s_kernel(tc, x, Ws1, bs1, Ws2, out):
+    nc = tc.nc
+    with ExitStack() as stack:
+        keep = stack.enter_context(tc.tile_pool(name="keep", bufs=1))
+        stage = stack.enter_context(tc.tile_pool(name="stage", bufs=3))
+        small = stack.enter_context(tc.tile_pool(name="small", bufs=2))
+        flip_psum = stack.enter_context(tc.psum_pool(name="flip", bufs=3))
+        hidden_psum = stack.enter_context(tc.psum_pool(name="hidden", bufs=2))
+        sink_psum = stack.enter_context(tc.psum_pool(name="sink", bufs=1))
+
+        x_raw = keep.tile([P, K], BF16)
+        nc.sync.dma_start(
+            out=x_raw[:].rearrange("q (a f) -> q a f", a=IMAGES * PASSES * HALVES),
+            in_=x.rearrange("b (a q e) h w -> q (b a) (e h w)", a=PASSES * HALVES, e=2),
+        )
+        bias_bf = keep.tile([P, ROW_TILES], BF16)
+        nc.scalar.dma_start(
+            out=bias_bf[:].rearrange("p (a e) -> p a e", e=2),
+            in_=bs1.rearrange("(a p e) -> p a e", a=PASSES * HALVES, e=2),
+        )
+        w1_rows = keep.tile([P, ROW_TILES, K], BF16)
+        w2_rows = keep.tile([P, K], BF16)
+        w1_view = Ws1.rearrange("(a p e) c -> a e p c", a=PASSES * HALVES, e=2)
+        for i in range(ROW_TILES):
+            if i == W2_TURN:
+                nc.sync.dma_start(out=w2_rows[:], in_=Ws2)
+            nc.sync.dma_start(out=w1_rows[:, i, :], in_=w1_view[i // 2, i % 2])
+
+        ident = keep.tile([P, P], F32)
+        make_identity(nc, ident[:])
+        mean_of_pixels = keep.tile([P, P], F32)
+        nc.vector.memset(mean_of_pixels[:], 1.0 / PIXELS)
+        col_factor = keep.tile([P, IMAGES], F32)
+        nc.vector.memset(col_factor[:], 0.0)
+        warm = keep.tile([P, 1], F32)
+        nc.vector.memset(warm[:], 0.0)
+        nc.scalar.activation(out=warm[:], in_=warm[:], func=ACT.Exp)
+        bias = keep.tile([P, ROW_TILES], F32)
+        nc.vector.tensor_copy(out=bias[:], in_=bias_bf[:])
+
+        x_grouped = keep.tile([P, K], BF16, align_bytes=64)
+        x_codes = keep.tile([P, PASSES, COLS], U32, align_bytes=64)
+        x_scales = keep.tile([P, PASSES, COLS], U8, align_bytes=64)
+        x_from = x_raw[:].rearrange("q (b g t n) -> q g b n t", b=IMAGES, g=PASSES, t=PACK)
+        x_to = x_grouped[:].rearrange("q (g b n t) -> q g b n t", g=PASSES, b=IMAGES, t=PACK)
+        for g in range(PASSES):
+            nc.vector.tensor_copy(out=x_to[:, g], in_=x_from[:, g])
+        nc.vector.quantize_mx(
+            out=x_codes[:].rearrange("q g c -> q (g c)").bitcast(FP8X4),
+            scales=x_scales[:].rearrange("q g c -> q (g c)"),
+            in_=x_grouped[:],
+        )
+
+        def flip_and_quantise(rows, codes, scales, copy):
+            words = rows.bitcast(F32)
+            flipped = flip_psum.tile([P, PASSES * HALVES * P], F32, tag="flipped")
+            for a in range(PASSES * HALVES):
+                nc.tensor.transpose(flipped[:, a * P : (a + 1) * P], words[:, a * P : (a + 1) * P], ident[:])
+            grouped = stage.tile([P, K], BF16, align_bytes=64)
+            copy(
+                out=grouped[:].bitcast(F32).rearrange("q (g r u) -> q g r u", g=PASSES, u=HALVES),
+                in_=flipped[:].rearrange("q (g u r) -> q g r u", g=PASSES, u=HALVES),
+            )
+            nc.vector.quantize_mx(
+                out=codes.rearrange("q g r -> q (g r)").bitcast(FP8X4),
+                scales=scales.rearrange("q g r -> q (g r)"),
+                in_=grouped[:],
+            )
+
+        w1_codes = keep.tile([P, ROW_TILES, PASSES, P], U32, align_bytes=64)
+        w1_scales = keep.tile([P, ROW_TILES, PASSES, P], U8, align_bytes=64)
+        w2_codes = keep.tile([P, PASSES, P], U32, align_bytes=64)
+        w2_scales = keep.tile([P, PASSES, P], U8, align_bytes=64)
+        hs_grouped = keep.tile([P, K], BF16, align_bytes=64)
+        hs_view = hs_grouped[:].rearrange("p (g c t) -> p g c t", g=PASSES, t=PACK)
+        hs_codes = keep.tile([P, PASSES, COLS], U32, align_bytes=64)
+        hs_scales = keep.tile([P, PASSES, COLS], U8, align_bytes=64)
+        scores = sink_psum.tile([P, COLS], F32, tag="scores")
+
+        for i in range(ROW_TILES):
+            if i == W2_TURN:
+                flip_and_quantise(w2_rows[:], w2_codes[:], w2_scales[:], nc.scalar.copy)
+            copy = nc.scalar.copy if i % 2 == 0 else nc.vector.tensor_copy
+            flip_and_quantise(w1_rows[:, i, :], w1_codes[:, i], w1_scales[:, i], copy)
+            hidden = hidden_psum.tile([P, COLS], F32)
+            for g in range(PASSES):
+                nc.tensor.matmul_mx(
+                    out=hidden[:],
+                    lhsT=w1_codes[:, i, g, :].bitcast(FP8X4),
+                    lhsT_scale=w1_scales[:, i, g, :],
+                    rhs=x_codes[:, g, :].bitcast(FP8X4),
+                    rhs_scale=x_scales[:, g, :],
+                    start=(g == 0),
+                    stop=(g == PASSES - 1),
+                )
+            nc.scalar.activation(
+                out=hs_view[:, i // PACK, :, i % PACK],
+                in_=hidden[:],
+                func=ACT.Relu,
+                bias=bias[:, i : i + 1],
+                scale=1.0,
+            )
+            if i % PACK == PACK - 1:
+                g = i // PACK
+                nc.vector.quantize_mx(
+                    out=hs_codes[:, g, :].bitcast(FP8X4),
+                    scales=hs_scales[:, g, :],
+                    in_=hs_grouped[:, g * COLS * PACK : (g + 1) * COLS * PACK],
+                )
+                nc.tensor.matmul_mx(
+                    out=scores[:],
+                    lhsT=w2_codes[:, g, :].bitcast(FP8X4),
+                    lhsT_scale=w2_scales[:, g, :],
+                    rhs=hs_codes[:, g, :].bitcast(FP8X4),
+                    rhs_scale=hs_scales[:, g, :],
+                    start=(g == 0),
+                    stop=(g == PASSES - 1),
+                )
+
+        neg_top = small.tile([P, IMAGES], F32)
+        nc.vector.tensor_reduce(
+            out=neg_top[:],
+            in_=scores[:].rearrange("m (b n) -> m b n", b=IMAGES),
+            axis=AXIS.X,
+            op=ALU.max,
+            negate=True,
+        )
+        kern = keep.tile([P, COLS], F32)
+        first_sums = small.tile([P, IMAGES], F32)
+        for b in range(IMAGES):
+            pixels = slice(b * PIXELS, (b + 1) * PIXELS)
+            nc.scalar.activation(
+                out=kern[:, pixels],
+                in_=scores[:, pixels],
+                func=ACT.Exp,
+                bias=neg_top[:, b : b + 1],
+                scale=1.0,
+                accum_out=first_sums[:, b : b + 1],
+            )
+        row_factor = small.tile([P, 2 * IMAGES], F32, tag="row_factor")
+        nc.vector.memset(row_factor[:, IMAGES:], 1.0)
+        nc.vector.reciprocal(out=row_factor[:, :IMAGES], in_=first_sums[:])
+
+        kern_flipped = flip_psum.tile([P, PASSES * HALVES * P], F32, tag="flipped")
+        nc.tensor.transpose(kern_flipped[:, :P], kern[:], ident[:])
+        kern_t = keep.tile([P, P], F32)
+        nc.scalar.copy(out=kern_t[:], in_=kern_flipped[:, :P])
+
+        last_col_factor = keep.tile([P, 1], F32)
+        for r in range(ROUNDS):
+            col_sums = sink_psum.tile([P, IMAGES], F32, tag="col_sums")
+            nc.tensor.matmul(out=col_sums[:], lhsT=kern[:], rhs=row_factor[:, :IMAGES], start=True, stop=False)
+            nc.tensor.matmul(out=col_sums[:], lhsT=ident[:], rhs=row_factor[:, IMAGES:], start=False, stop=True)
+            for b in range(IMAGES):
+                rows = slice(b * PIXELS, (b + 1) * PIXELS)
+                if r == ROUNDS - 1:
+                    nc.vector.reciprocal(out=last_col_factor[rows, :], in_=col_sums[rows, b : b + 1])
+                else:
+                    nc.vector.reciprocal(out=col_factor[rows, b : b + 1], in_=col_sums[rows, b : b + 1])
+            if r == ROUNDS - 1:
+                break
+            row_sums = sink_psum.tile([P, 2 * IMAGES], F32, tag="row_sums")
+            nc.tensor.matmul(out=row_sums[:, :IMAGES], lhsT=kern_t[:], rhs=col_factor[:], start=True, stop=True)
+            nc.tensor.matmul(out=row_sums[:, IMAGES:], lhsT=mean_of_pixels[:], rhs=col_factor[:], start=True, stop=True)
+            row_factor = small.tile([P, 2 * IMAGES], F32, tag="row_factor")
+            nc.vector.reciprocal(out=row_factor[:], in_=row_sums[:])
+
+        weighted = keep.tile([P, COLS], F32)
+        for b in range(IMAGES):
+            pixels = slice(b * PIXELS, (b + 1) * PIXELS)
+            nc.scalar.activation(
+                out=weighted[:, pixels], in_=kern[:, pixels], func=ACT.Copy, scale=row_factor[:, b : b + 1]
+            )
+        spread = flip_psum.tile([P, PASSES * HALVES * P], F32, tag="flipped")
+        nc.tensor.transpose(spread[:, :P], last_col_factor[:, 0:1].to_broadcast([P, P]), ident[:])
+        result = keep.tile([P, COLS], F32)
+        nc.vector.tensor_tensor(out=result[:], in0=weighted[:], in1=spread[:, :P], op=ALU.mult)
+        nc.sync.dma_start(
+            out=out.rearrange("b m n -> m b n"), in_=result[:].rearrange("m (b n) -> m b n", b=IMAGES)
+        )

@@ -21,8 +21,8 @@ PACK = 4
 PASSES = K // (P * PACK)
 HALVES = 2
 ROW_TILES = K // P
+RUN = 2
 ROUNDS = 3
-W2_TURN = 2
 
 FLOPS = 2 * K * K * COLS + 2 * P * K * COLS
 
@@ -30,30 +30,30 @@ FLOPS = 2 * K * K * COLS + 2 * P * K * COLS
 def tile_salad_pa_s_kernel(tc, x, Ws1, bs1, Ws2, out):
     nc = tc.nc
     with ExitStack() as stack:
+        stack.enter_context(tc.manual_schedule())
         keep = stack.enter_context(tc.tile_pool(name="keep", bufs=1))
-        stage = stack.enter_context(tc.tile_pool(name="stage", bufs=3))
+        stage = stack.enter_context(tc.tile_pool(name="stage", bufs=4))
         small = stack.enter_context(tc.tile_pool(name="small", bufs=2))
-        flip_psum = stack.enter_context(tc.psum_pool(name="flip", bufs=3))
-        hidden_psum = stack.enter_context(tc.psum_pool(name="hidden", bufs=2))
-        sink_psum = stack.enter_context(tc.psum_pool(name="sink", bufs=1))
+        banks = stack.enter_context(tc.psum_pool(name="banks", bufs=5))
+        held_banks = stack.enter_context(tc.psum_pool(name="held", bufs=1))
 
+        w1_rows = keep.tile([P, ROW_TILES, K], BF16)
+        w1_view = Ws1.rearrange("(a p e) c -> a e p c", a=PASSES * HALVES, e=2)
         x_raw = keep.tile([P, K], BF16)
-        nc.sync.dma_start(
-            out=x_raw[:].rearrange("q (a f) -> q a f", a=IMAGES * PASSES * HALVES),
-            in_=x.rearrange("b (a q e) h w -> q (b a) (e h w)", a=PASSES * HALVES, e=2),
-        )
+        w2_rows = keep.tile([P, K], BF16)
+        for i in range(ROW_TILES):
+            nc.sync.dma_start(out=w1_rows[:, i, :], in_=w1_view[i // 2, i % 2])
+            if i == 0:
+                nc.sync.dma_start(
+                    out=x_raw[:].rearrange("q (a f) -> q a f", a=IMAGES * PASSES * HALVES),
+                    in_=x.rearrange("b (a q e) h w -> q (b a) (e h w)", a=PASSES * HALVES, e=2),
+                )
+        nc.sync.dma_start(out=w2_rows[:], in_=Ws2)
         bias_bf = keep.tile([P, ROW_TILES], BF16)
         nc.scalar.dma_start(
             out=bias_bf[:].rearrange("p (a e) -> p a e", e=2),
             in_=bs1.rearrange("(a p e) -> p a e", a=PASSES * HALVES, e=2),
         )
-        w1_rows = keep.tile([P, ROW_TILES, K], BF16)
-        w2_rows = keep.tile([P, K], BF16)
-        w1_view = Ws1.rearrange("(a p e) c -> a e p c", a=PASSES * HALVES, e=2)
-        for i in range(ROW_TILES):
-            if i == W2_TURN:
-                nc.sync.dma_start(out=w2_rows[:], in_=Ws2)
-            nc.sync.dma_start(out=w1_rows[:, i, :], in_=w1_view[i // 2, i % 2])
 
         ident = keep.tile([P, P], F32)
         make_identity(nc, ident[:])
@@ -61,11 +61,27 @@ def tile_salad_pa_s_kernel(tc, x, Ws1, bs1, Ws2, out):
         nc.vector.memset(mean_of_pixels[:], 1.0 / PIXELS)
         col_factor = keep.tile([P, IMAGES], F32)
         nc.vector.memset(col_factor[:], 0.0)
+        ones = keep.tile([P, IMAGES], F32)
+        nc.vector.memset(ones[:], 1.0)
         warm = keep.tile([P, 1], F32)
         nc.vector.memset(warm[:], 0.0)
         nc.scalar.activation(out=warm[:], in_=warm[:], func=ACT.Exp)
-        bias = keep.tile([P, ROW_TILES], F32)
-        nc.vector.tensor_copy(out=bias[:], in_=bias_bf[:])
+
+        def flip_and_quantise(rows, codes, scales):
+            words = rows.bitcast(F32)
+            flipped = banks.tile([P, PASSES * HALVES * P], F32, tag="bank")
+            for a in range(PASSES * HALVES):
+                nc.tensor.transpose(flipped[:, a * P : (a + 1) * P], words[:, a * P : (a + 1) * P], ident[:])
+            grouped = stage.tile([P, K], BF16, align_bytes=64)
+            nc.scalar.copy(
+                out=grouped[:].bitcast(F32).rearrange("q (g r u) -> q g r u", g=PASSES, u=HALVES),
+                in_=flipped[:].rearrange("q (g u r) -> q g r u", g=PASSES, u=HALVES),
+            )
+            nc.vector.quantize_mx(
+                out=codes.rearrange("q g r -> q (g r)").bitcast(FP8X4),
+                scales=scales.rearrange("q g r -> q (g r)"),
+                in_=grouped[:],
+            )
 
         x_grouped = keep.tile([P, K], BF16, align_bytes=64)
         x_codes = keep.tile([P, PASSES, COLS], U32, align_bytes=64)
@@ -79,42 +95,20 @@ def tile_salad_pa_s_kernel(tc, x, Ws1, bs1, Ws2, out):
             scales=x_scales[:].rearrange("q g c -> q (g c)"),
             in_=x_grouped[:],
         )
-
-        def flip_and_quantise(rows, codes, scales, copy):
-            words = rows.bitcast(F32)
-            flipped = flip_psum.tile([P, PASSES * HALVES * P], F32, tag="flipped")
-            for a in range(PASSES * HALVES):
-                nc.tensor.transpose(flipped[:, a * P : (a + 1) * P], words[:, a * P : (a + 1) * P], ident[:])
-            grouped = stage.tile([P, K], BF16, align_bytes=64)
-            copy(
-                out=grouped[:].bitcast(F32).rearrange("q (g r u) -> q g r u", g=PASSES, u=HALVES),
-                in_=flipped[:].rearrange("q (g u r) -> q g r u", g=PASSES, u=HALVES),
-            )
-            nc.vector.quantize_mx(
-                out=codes.rearrange("q g r -> q (g r)").bitcast(FP8X4),
-                scales=scales.rearrange("q g r -> q (g r)"),
-                in_=grouped[:],
-            )
+        w2_codes = keep.tile([P, PASSES, P], U32, align_bytes=64)
+        w2_scales = keep.tile([P, PASSES, P], U8, align_bytes=64)
 
         w1_codes = keep.tile([P, ROW_TILES, PASSES, P], U32, align_bytes=64)
         w1_scales = keep.tile([P, ROW_TILES, PASSES, P], U8, align_bytes=64)
-        w2_codes = keep.tile([P, PASSES, P], U32, align_bytes=64)
-        w2_scales = keep.tile([P, PASSES, P], U8, align_bytes=64)
-        hs_grouped = keep.tile([P, K], BF16, align_bytes=64)
-        hs_view = hs_grouped[:].rearrange("p (g c t) -> p g c t", g=PASSES, t=PACK)
         hs_codes = keep.tile([P, PASSES, COLS], U32, align_bytes=64)
         hs_scales = keep.tile([P, PASSES, COLS], U8, align_bytes=64)
-        scores = sink_psum.tile([P, COLS], F32, tag="scores")
+        hidden = [held_banks.tile([P, PACK, COLS], F32, name="hidden%d" % g) for g in range(PASSES)]
+        scores = held_banks.tile([P, COLS], F32)
 
-        for i in range(ROW_TILES):
-            if i == W2_TURN:
-                flip_and_quantise(w2_rows[:], w2_codes[:], w2_scales[:], nc.scalar.copy)
-            copy = nc.scalar.copy if i % 2 == 0 else nc.vector.tensor_copy
-            flip_and_quantise(w1_rows[:, i, :], w1_codes[:, i], w1_scales[:, i], copy)
-            hidden = hidden_psum.tile([P, COLS], F32)
+        def first_product(i):
             for g in range(PASSES):
                 nc.tensor.matmul_mx(
-                    out=hidden[:],
+                    out=hidden[i // PACK][:, i % PACK, :],
                     lhsT=w1_codes[:, i, g, :].bitcast(FP8X4),
                     lhsT_scale=w1_scales[:, i, g, :],
                     rhs=x_codes[:, g, :].bitcast(FP8X4),
@@ -122,30 +116,46 @@ def tile_salad_pa_s_kernel(tc, x, Ws1, bs1, Ws2, out):
                     start=(g == 0),
                     stop=(g == PASSES - 1),
                 )
-            nc.scalar.activation(
-                out=hs_view[:, i // PACK, :, i % PACK],
-                in_=hidden[:],
-                func=ACT.Relu,
-                bias=bias[:, i : i + 1],
-                scale=1.0,
-            )
-            if i % PACK == PACK - 1:
-                g = i // PACK
-                nc.vector.quantize_mx(
-                    out=hs_codes[:, g, :].bitcast(FP8X4),
-                    scales=hs_scales[:, g, :],
-                    in_=hs_grouped[:, g * COLS * PACK : (g + 1) * COLS * PACK],
-                )
-                nc.tensor.matmul_mx(
-                    out=scores[:],
-                    lhsT=w2_codes[:, g, :].bitcast(FP8X4),
-                    lhsT_scale=w2_scales[:, g, :],
-                    rhs=hs_codes[:, g, :].bitcast(FP8X4),
-                    rhs_scale=hs_scales[:, g, :],
-                    start=(g == 0),
-                    stop=(g == PASSES - 1),
-                )
 
+        def quantise_hidden(g):
+            summed = stage.tile([P, COLS * PACK], BF16)
+            nc.vector.tensor_tensor(
+                out=summed[:].rearrange("p (c t) -> p c t", t=PACK),
+                in0=hidden[g][:].rearrange("p t c -> p c t"),
+                in1=bias_bf[:, g * PACK : (g + 1) * PACK].unsqueeze(1).to_broadcast([P, COLS, PACK]),
+                op=ALU.add,
+            )
+            hs_grouped = stage.tile([P, COLS * PACK], BF16, align_bytes=64)
+            nc.vector.tensor_scalar_max(out=hs_grouped[:], in0=summed[:], scalar1=0.0)
+            nc.vector.quantize_mx(
+                out=hs_codes[:, g, :].bitcast(FP8X4), scales=hs_scales[:, g, :], in_=hs_grouped[:]
+            )
+
+        def second_product(g):
+            nc.tensor.matmul_mx(
+                out=scores[:],
+                lhsT=w2_codes[:, g, :].bitcast(FP8X4),
+                lhsT_scale=w2_scales[:, g, :],
+                rhs=hs_codes[:, g, :].bitcast(FP8X4),
+                rhs_scale=hs_scales[:, g, :],
+                start=(g == 0),
+                stop=(g == PASSES - 1),
+            )
+
+        for first in range(0, ROW_TILES + RUN, RUN):
+            for i in range(first, min(first + RUN, ROW_TILES)):
+                flip_and_quantise(w1_rows[:, i, :], w1_codes[:, i], w1_scales[:, i])
+            if first == ROW_TILES:
+                flip_and_quantise(w2_rows[:], w2_codes[:], w2_scales[:])
+            for i in range(max(first - RUN, 0), first):
+                first_product(i)
+                if i % PACK == PACK - 1:
+                    quantise_hidden(i // PACK)
+        for g in range(PASSES):
+            second_product(g)
+
+        col_sums = banks.tile([P, IMAGES], F32, tag="bank")
+        nc.tensor.matmul(out=col_sums[:], lhsT=ident[:], rhs=ones[:], start=True, stop=False)
         neg_top = small.tile([P, IMAGES], F32)
         nc.vector.tensor_reduce(
             out=neg_top[:],
@@ -166,20 +176,17 @@ def tile_salad_pa_s_kernel(tc, x, Ws1, bs1, Ws2, out):
                 scale=1.0,
                 accum_out=first_sums[:, b : b + 1],
             )
-        row_factor = small.tile([P, 2 * IMAGES], F32, tag="row_factor")
-        nc.vector.memset(row_factor[:, IMAGES:], 1.0)
-        nc.vector.reciprocal(out=row_factor[:, :IMAGES], in_=first_sums[:])
+        row_factor = small.tile([P, IMAGES], F32, tag="row_factor")
+        nc.vector.reciprocal(out=row_factor[:], in_=first_sums[:])
 
-        kern_flipped = flip_psum.tile([P, PASSES * HALVES * P], F32, tag="flipped")
-        nc.tensor.transpose(kern_flipped[:, :P], kern[:], ident[:])
+        kern_flipped = banks.tile([P, P], F32, tag="bank")
+        nc.tensor.transpose(kern_flipped[:], kern[:], ident[:])
         kern_t = keep.tile([P, P], F32)
-        nc.scalar.copy(out=kern_t[:], in_=kern_flipped[:, :P])
+        nc.scalar.copy(out=kern_t[:], in_=kern_flipped[:])
 
         last_col_factor = keep.tile([P, 1], F32)
         for r in range(ROUNDS):
-            col_sums = sink_psum.tile([P, IMAGES], F32, tag="col_sums")
-            nc.tensor.matmul(out=col_sums[:], lhsT=kern[:], rhs=row_factor[:, :IMAGES], start=True, stop=False)
-            nc.tensor.matmul(out=col_sums[:], lhsT=ident[:], rhs=row_factor[:, IMAGES:], start=False, stop=True)
+            nc.tensor.matmul(out=col_sums[:], lhsT=kern[:], rhs=row_factor[:], start=False, stop=True)
             for b in range(IMAGES):
                 rows = slice(b * PIXELS, (b + 1) * PIXELS)
                 if r == ROUNDS - 1:
@@ -188,10 +195,15 @@ def tile_salad_pa_s_kernel(tc, x, Ws1, bs1, Ws2, out):
                     nc.vector.reciprocal(out=col_factor[rows, b : b + 1], in_=col_sums[rows, b : b + 1])
             if r == ROUNDS - 1:
                 break
-            row_sums = sink_psum.tile([P, 2 * IMAGES], F32, tag="row_sums")
-            nc.tensor.matmul(out=row_sums[:, :IMAGES], lhsT=kern_t[:], rhs=col_factor[:], start=True, stop=True)
-            nc.tensor.matmul(out=row_sums[:, IMAGES:], lhsT=mean_of_pixels[:], rhs=col_factor[:], start=True, stop=True)
-            row_factor = small.tile([P, 2 * IMAGES], F32, tag="row_factor")
+            dust_sums = banks.tile([P, IMAGES], F32, tag="bank")
+            nc.tensor.matmul(out=dust_sums[:], lhsT=mean_of_pixels[:], rhs=col_factor[:], start=True, stop=True)
+            row_sums = banks.tile([P, IMAGES], F32, tag="bank")
+            nc.tensor.matmul(out=row_sums[:], lhsT=kern_t[:], rhs=col_factor[:], start=True, stop=True)
+            dust_factor = small.tile([P, IMAGES], F32, tag="dust_factor")
+            nc.vector.reciprocal(out=dust_factor[:], in_=dust_sums[:])
+            col_sums = banks.tile([P, IMAGES], F32, tag="bank")
+            nc.tensor.matmul(out=col_sums[:], lhsT=ident[:], rhs=dust_factor[:], start=True, stop=False)
+            row_factor = small.tile([P, IMAGES], F32, tag="row_factor")
             nc.vector.reciprocal(out=row_factor[:], in_=row_sums[:])
 
         weighted = keep.tile([P, COLS], F32)
@@ -200,10 +212,10 @@ def tile_salad_pa_s_kernel(tc, x, Ws1, bs1, Ws2, out):
             nc.scalar.activation(
                 out=weighted[:, pixels], in_=kern[:, pixels], func=ACT.Copy, scale=row_factor[:, b : b + 1]
             )
-        spread = flip_psum.tile([P, PASSES * HALVES * P], F32, tag="flipped")
-        nc.tensor.transpose(spread[:, :P], last_col_factor[:, 0:1].to_broadcast([P, P]), ident[:])
+        spread = banks.tile([P, P], F32, tag="bank")
+        nc.tensor.transpose(spread[:], last_col_factor[:, 0:1].to_broadcast([P, P]), ident[:])
         result = keep.tile([P, COLS], F32)
-        nc.vector.tensor_tensor(out=result[:], in0=weighted[:], in1=spread[:, :P], op=ALU.mult)
+        nc.vector.tensor_tensor(out=result[:], in0=weighted[:], in1=spread[:], op=ALU.mult)
         nc.sync.dma_start(
             out=out.rearrange("b m n -> m b n"), in_=result[:].rearrange("m (b n) -> m b n", b=IMAGES)
         )

@@ -23,6 +23,8 @@ HALVES = 2
 ROW_TILES = K // P
 RUN = 2
 ROUNDS = 3
+WARM_UP = 6
+BANK = 512
 
 FLOPS = 2 * K * K * COLS + 2 * P * K * COLS
 
@@ -54,6 +56,23 @@ def tile_salad_pa_s_kernel(tc, x, Ws1, bs1, Ws2, out):
             out=bias_bf[:].rearrange("p (a e) -> p a e", e=2),
             in_=bs1.rearrange("(a p e) -> p a e", a=PASSES * HALVES, e=2),
         )
+
+        idle_data = keep.tile([P, BANK * PACK], BF16, align_bytes=64)
+        idle_codes = keep.tile([P, BANK], U32, align_bytes=64)
+        idle_scales = keep.tile([P, BANK], U8, align_bytes=64)
+        nc.vector.memset(idle_data[:], 0.0)
+        nc.vector.quantize_mx(out=idle_codes[:].bitcast(FP8X4), scales=idle_scales[:], in_=idle_data[:])
+        idle_bank = banks.tile([P, BANK], F32, tag="bank")
+        for w in range(WARM_UP):
+            nc.tensor.matmul_mx(
+                out=idle_bank[:],
+                lhsT=idle_codes[:, :P].bitcast(FP8X4),
+                lhsT_scale=idle_scales[:, :P],
+                rhs=idle_codes[:].bitcast(FP8X4),
+                rhs_scale=idle_scales[:],
+                start=True,
+                stop=True,
+            )
 
         ident = keep.tile([P, P], F32)
         make_identity(nc, ident[:])

@@ -21,10 +21,8 @@ PACK = 4
 PASSES = K // (P * PACK)
 HALVES = 2
 ROW_TILES = K // P
-RUN = 2
+LEAD = 2
 ROUNDS = 3
-WARM_UP = 6
-BANK = 512
 
 FLOPS = 2 * K * K * COLS + 2 * P * K * COLS
 
@@ -56,23 +54,6 @@ def tile_salad_pa_s_kernel(tc, x, Ws1, bs1, Ws2, out):
             out=bias_bf[:].rearrange("p (a e) -> p a e", e=2),
             in_=bs1.rearrange("(a p e) -> p a e", a=PASSES * HALVES, e=2),
         )
-
-        idle_data = keep.tile([P, BANK * PACK], BF16, align_bytes=64)
-        idle_codes = keep.tile([P, BANK], U32, align_bytes=64)
-        idle_scales = keep.tile([P, BANK], U8, align_bytes=64)
-        nc.vector.memset(idle_data[:], 0.0)
-        nc.vector.quantize_mx(out=idle_codes[:].bitcast(FP8X4), scales=idle_scales[:], in_=idle_data[:])
-        idle_bank = banks.tile([P, BANK], F32, tag="bank")
-        for w in range(WARM_UP):
-            nc.tensor.matmul_mx(
-                out=idle_bank[:],
-                lhsT=idle_codes[:, :P].bitcast(FP8X4),
-                lhsT_scale=idle_scales[:, :P],
-                rhs=idle_codes[:].bitcast(FP8X4),
-                rhs_scale=idle_scales[:],
-                start=True,
-                stop=True,
-            )
 
         ident = keep.tile([P, P], F32)
         make_identity(nc, ident[:])
@@ -161,15 +142,17 @@ def tile_salad_pa_s_kernel(tc, x, Ws1, bs1, Ws2, out):
                 stop=(g == PASSES - 1),
             )
 
-        for first in range(0, ROW_TILES + RUN, RUN):
-            for i in range(first, min(first + RUN, ROW_TILES)):
-                flip_and_quantise(w1_rows[:, i, :], w1_codes[:, i], w1_scales[:, i])
-            if first == ROW_TILES:
-                flip_and_quantise(w2_rows[:], w2_codes[:], w2_scales[:])
-            for i in range(max(first - RUN, 0), first):
-                first_product(i)
-                if i % PACK == PACK - 1:
-                    quantise_hidden(i // PACK)
+        to_flip = [(w1_rows[:, i, :], w1_codes[:, i], w1_scales[:, i]) for i in range(ROW_TILES)]
+        to_flip.append((w2_rows[:], w2_codes[:], w2_scales[:]))
+        n_flipped = 0
+        for g in range(PASSES):
+            ahead = min((g + 1) * PACK + LEAD, len(to_flip))
+            for rows, codes, scales in to_flip[n_flipped:ahead]:
+                flip_and_quantise(rows, codes, scales)
+            n_flipped = ahead
+            for t in range(PACK):
+                first_product(g * PACK + t)
+            quantise_hidden(g)
         for g in range(PASSES):
             second_product(g)
 

from contextlib import ExitStack

import concourse.mybir as mybir
from concourse.masks import make_identity

F32 = mybir.dt.float32
BF16 = mybir.dt.bfloat16
U32 = mybir.dt.uint32
U8 = mybir.dt.uint8
FP8X4 = mybir.dt.float8_e4m3fn_x4
ACT = mybir.ActivationFunctionType
ALU = mybir.AluOpType
AXIS = mybir.AxisListType

P = 128
IMAGES = 2
PIXELS = 64
COLS = IMAGES * PIXELS
K = 1024
PACK = 4
PASSES = K // (P * PACK)
HALVES = 2
ROW_TILES = K // P
LEAD = 2
ROUNDS = 3

FLOPS = 2 * K * K * COLS + 2 * P * K * COLS


def tile_salad_pa_s_kernel(tc, x, Ws1, bs1, Ws2, out):
    nc = tc.nc
    with ExitStack() as stack:
        stack.enter_context(tc.manual_schedule())
        keep = stack.enter_context(tc.tile_pool(name="keep", bufs=1))
        stage = stack.enter_context(tc.tile_pool(name="stage", bufs=4))
        small = stack.enter_context(tc.tile_pool(name="small", bufs=2))
        banks = stack.enter_context(tc.psum_pool(name="banks", bufs=5))
        held_banks = stack.enter_context(tc.psum_pool(name="held", bufs=1))

        w1_rows = keep.tile([P, ROW_TILES, K], BF16)
        w1_view = Ws1.rearrange("(a p e) c -> a e p c", a=PASSES * HALVES, e=2)
        x_raw = keep.tile([P, K], BF16)
        w2_rows = keep.tile([P, K], BF16)
        for i in range(ROW_TILES):
            nc.sync.dma_start(out=w1_rows[:, i, :], in_=w1_view[i // 2, i % 2])
            if i == 0:
                nc.sync.dma_start(
                    out=x_raw[:].rearrange("q (a f) -> q a f", a=IMAGES * PASSES * HALVES),
                    in_=x.rearrange("b (a q e) h w -> q (b a) (e h w)", a=PASSES * HALVES, e=2),
                )
        nc.sync.dma_start(out=w2_rows[:], in_=Ws2)
        bias_bf = keep.tile([P, ROW_TILES], BF16)
        nc.scalar.dma_start(
            out=bias_bf[:].rearrange("p (a e) -> p a e", e=2),
            in_=bs1.rearrange("(a p e) -> p a e", a=PASSES * HALVES, e=2),
        )

        ident = keep.tile([P, P], F32)
        make_identity(nc, ident[:])
        mean_of_pixels = keep.tile([P, P], F32)
        nc.vector.memset(mean_of_pixels[:], 1.0 / PIXELS)
        col_factor = keep.tile([P, IMAGES], F32)
        nc.vector.memset(col_factor[:], 0.0)
        ones = keep.tile([P, IMAGES], F32)
        nc.vector.memset(ones[:], 1.0)
        warm = keep.tile([P, 1], F32)
        nc.vector.memset(warm[:], 0.0)
        nc.scalar.activation(out=warm[:], in_=warm[:], func=ACT.Exp)

        def flip_and_quantise(rows, codes, scales):
            words = rows.bitcast(F32)
            flipped = banks.tile([P, PASSES * HALVES * P], F32, tag="bank")
            for a in range(PASSES * HALVES):
                nc.tensor.transpose(flipped[:, a * P : (a + 1) * P], words[:, a * P : (a + 1) * P], ident[:])
            grouped = stage.tile([P, K], BF16, align_bytes=64)
            nc.scalar.copy(
                out=grouped[:].bitcast(F32).rearrange("q (g r u) -> q g r u", g=PASSES, u=HALVES),
                in_=flipped[:].rearrange("q (g u r) -> q g r u", g=PASSES, u=HALVES),
            )
            nc.vector.quantize_mx(
                out=codes.rearrange("q g r -> q (g r)").bitcast(FP8X4),
                scales=scales.rearrange("q g r -> q (g r)"),
                in_=grouped[:],
            )

        x_grouped = keep.tile([P, K], BF16, align_bytes=64)
        x_codes = keep.tile([P, PASSES, COLS], U32, align_bytes=64)
        x_scales = keep.tile([P, PASSES, COLS], U8, align_bytes=64)
        x_from = x_raw[:].rearrange("q (b g t n) -> q g b n t", b=IMAGES, g=PASSES, t=PACK)
        x_to = x_grouped[:].rearrange("q (g b n t) -> q g b n t", g=PASSES, b=IMAGES, t=PACK)
        for g in range(PASSES):
            nc.vector.tensor_copy(out=x_to[:, g], in_=x_from[:, g])
        nc.vector.quantize_mx(
            out=x_codes[:].rearrange("q g c -> q (g c)").bitcast(FP8X4),
            scales=x_scales[:].rearrange("q g c -> q (g c)"),
            in_=x_grouped[:],
        )
        w2_codes = keep.tile([P, PASSES, P], U32, align_bytes=64)
        w2_scales = keep.tile([P, PASSES, P], U8, align_bytes=64)

        w1_codes = keep.tile([P, ROW_TILES, PASSES, P], U32, align_bytes=64)
        w1_scales = keep.tile([P, ROW_TILES, PASSES, P], U8, align_bytes=64)
        hs_codes = keep.tile([P, PASSES, COLS], U32, align_bytes=64)
        hs_scales = keep.tile([P, PASSES, COLS], U8, align_bytes=64)
        hidden = [held_banks.tile([P, PACK, COLS], F32, name="hidden%d" % g) for g in range(PASSES)]
        scores = held_banks.tile([P, COLS], F32)

        def first_product(i):
            for g in range(PASSES):
                nc.tensor.matmul_mx(
                    out=hidden[i // PACK][:, i % PACK, :],
                    lhsT=w1_codes[:, i, g, :].bitcast(FP8X4),
                    lhsT_scale=w1_scales[:, i, g, :],
                    rhs=x_codes[:, g, :].bitcast(FP8X4),
                    rhs_scale=x_scales[:, g, :],
                    start=(g == 0),
                    stop=(g == PASSES - 1),
                )

        def quantise_hidden(g):
            summed = stage.tile([P, COLS * PACK], BF16)
            nc.vector.tensor_tensor(
                out=summed[:].rearrange("p (c t) -> p c t", t=PACK),
                in0=hidden[g][:].rearrange("p t c -> p c t"),
                in1=bias_bf[:, g * PACK : (g + 1) * PACK].unsqueeze(1).to_broadcast([P, COLS, PACK]),
                op=ALU.add,
            )
            hs_grouped = stage.tile([P, COLS * PACK], BF16, align_bytes=64)
            nc.vector.tensor_scalar_max(out=hs_grouped[:], in0=summed[:], scalar1=0.0)
            nc.vector.quantize_mx(
                out=hs_codes[:, g, :].bitcast(FP8X4), scales=hs_scales[:, g, :], in_=hs_grouped[:]
            )

        def second_product(g):
            nc.tensor.matmul_mx(
                out=scores[:],
                lhsT=w2_codes[:, g, :].bitcast(FP8X4),
                lhsT_scale=w2_scales[:, g, :],
                rhs=hs_codes[:, g, :].bitcast(FP8X4),
                rhs_scale=hs_scales[:, g, :],
                start=(g == 0),
                stop=(g == PASSES - 1),
            )

        to_flip = [(w1_rows[:, i, :], w1_codes[:, i], w1_scales[:, i]) for i in range(ROW_TILES)]
        to_flip.append((w2_rows[:], w2_codes[:], w2_scales[:]))
        n_flipped = 0
        for g in range(PASSES):
            ahead = min((g + 1) * PACK + LEAD, len(to_flip))
            for rows, codes, scales in to_flip[n_flipped:ahead]:
                flip_and_quantise(rows, codes, scales)
            n_flipped = ahead
            for t in range(PACK):
                first_product(g * PACK + t)
            quantise_hidden(g)
        for g in range(PASSES):
            second_product(g)

        col_sums = banks.tile([P, IMAGES], F32, tag="bank")
        nc.tensor.matmul(out=col_sums[:], lhsT=ident[:], rhs=ones[:], start=True, stop=False)
        neg_top = small.tile([P, IMAGES], F32)
        nc.vector.tensor_reduce(
            out=neg_top[:],
            in_=scores[:].rearrange("m (b n) -> m b n", b=IMAGES),
            axis=AXIS.X,
            op=ALU.max,
            negate=True,
        )
        kern = keep.tile([P, COLS], F32)
        first_sums = small.tile([P, IMAGES], F32)
        for b in range(IMAGES):
            pixels = slice(b * PIXELS, (b + 1) * PIXELS)
            nc.scalar.activation(
                out=kern[:, pixels],
                in_=scores[:, pixels],
                func=ACT.Exp,
                bias=neg_top[:, b : b + 1],
                scale=1.0,
                accum_out=first_sums[:, b : b + 1],
            )
        row_factor = small.tile([P, IMAGES], F32, tag="row_factor")
        nc.vector.reciprocal(out=row_factor[:], in_=first_sums[:])

        kern_flipped = banks.tile([P, P], F32, tag="bank")
        nc.tensor.transpose(kern_flipped[:], kern[:], ident[:])
        kern_t = keep.tile([P, P], F32)
        nc.scalar.copy(out=kern_t[:], in_=kern_flipped[:])

        last_col_factor = keep.tile([P, 1], F32)
        for r in range(ROUNDS):
            nc.tensor.matmul(out=col_sums[:], lhsT=kern[:], rhs=row_factor[:], start=False, stop=True)
            for b in range(IMAGES):
                rows = slice(b * PIXELS, (b + 1) * PIXELS)
                if r == ROUNDS - 1:
                    nc.vector.reciprocal(out=last_col_factor[rows, :], in_=col_sums[rows, b : b + 1])
                else:
                    nc.vector.reciprocal(out=col_factor[rows, b : b + 1], in_=col_sums[rows, b : b + 1])
            if r == ROUNDS - 1:
                break
            dust_sums = banks.tile([P, IMAGES], F32, tag="bank")
            nc.tensor.matmul(out=dust_sums[:], lhsT=mean_of_pixels[:], rhs=col_factor[:], start=True, stop=True)
            row_sums = banks.tile([P, IMAGES], F32, tag="bank")
            nc.tensor.matmul(out=row_sums[:], lhsT=kern_t[:], rhs=col_factor[:], start=True, stop=True)
            dust_factor = small.tile([P, IMAGES], F32, tag="dust_factor")
            nc.vector.reciprocal(out=dust_factor[:], in_=dust_sums[:])
            col_sums = banks.tile([P, IMAGES], F32, tag="bank")
            nc.tensor.matmul(out=col_sums[:], lhsT=ident[:], rhs=dust_factor[:], start=True, stop=False)
            row_factor = small.tile([P, IMAGES], F32, tag="row_factor")
            nc.vector.reciprocal(out=row_factor[:], in_=row_sums[:])

        weighted = keep.tile([P, COLS], F32)
        for b in range(IMAGES):
            pixels = slice(b * PIXELS, (b + 1) * PIXELS)
            nc.scalar.activation(
                out=weighted[:, pixels], in_=kern[:, pixels], func=ACT.Copy, scale=row_factor[:, b : b + 1]
            )
        spread = banks.tile([P, P], F32, tag="bank")
        nc.tensor.transpose(spread[:], last_col_factor[:, 0:1].to_broadcast([P, P]), ident[:])
        result = keep.tile([P, COLS], F32)
        nc.vector.tensor_tensor(out=result[:], in0=weighted[:], in1=spread[:], op=ALU.mult)
        nc.sync.dma_start(
            out=out.rearrange("b m n -> m b n"), in_=result[:].rearrange("m (b n) -> m b n", b=IMAGES)
        )
